import numpy as np
import ml_dtypes


def mxq(x, axis, fmt="e4m3"):
    dtype, down = {"e4m3": (ml_dtypes.float8_e4m3fn, 7), "e5m2": (ml_dtypes.float8_e5m2, 14)}[fmt]
    v = np.moveaxis(np.asarray(x, np.float32).astype(ml_dtypes.bfloat16).astype(np.float64), axis, -1)
    blocks = v.reshape(v.shape[:-1] + (-1, 32))
    amax = np.abs(blocks).max(-1, keepdims=True)
    byte = np.maximum(np.where(amax > 0, np.frexp(amax)[1] - 1 + 127, 0) - down, 1)
    scale = np.exp2(byte - 127.0)
    codes = (blocks / scale).astype(np.float32).astype(dtype).astype(np.float64)
    return np.moveaxis((codes * scale).reshape(v.shape), -1, axis)


WIDE = False


def mx_kscale(k):
    if not WIDE:
        return np.ones(k)
    levels = np.array([10, -10, 5, -5, 0])
    a = np.random.permutation(np.resize(levels, k // 512 * 4)).reshape(k // 512, 4)
    idx = np.arange(k)
    return np.exp2(a[idx // 512, idx % 128 // 32])


BF16 = ml_dtypes.bfloat16


def bf(x):
    return np.asarray(x, np.float32).astype(BF16)


def f64(x):
    return np.asarray(x).astype(np.float64)


B, C, H, W, K, R = 4, 1024, 32, 32, 1024, 8
EPS = 1e-8


def setup_inputs():
    s = mx_kscale(C)
    core = np.random.standard_normal((R, C)) / np.sqrt(R)
    fa = np.random.standard_normal((B, R, H, W))
    pa = np.random.standard_normal((K, R))
    features = 0.5 * np.random.standard_normal((B, C, H, W))
    prototypes = 0.5 * np.random.standard_normal((K, C))
    for r in range(R):
        features += core[r][None, :, None, None] * fa[:, r][:, None]
        prototypes += pa[:, r][:, None] * core[r][None, :]
    t = s[np.random.randint(0, C, (B, 1, H, W))]
    u = s[np.random.randint(0, C, (K, 1))]
    return {"features": bf(features * t), "prototypes": bf(prototypes * 0.5 / np.sqrt(C) * u)}


def reference(features, prototypes):
    f = f64(features).reshape(B, C, H * W).transpose(0, 2, 1)
    p = f64(prototypes)
    dots = mxq(f, 2, "e4m3") @ mxq(p, 1, "e4m3").T
    f_norm = np.linalg.norm(f, axis=-1)
    p_norm = np.linalg.norm(p, axis=-1)
    denom = np.maximum(f_norm[:, :, None] * p_norm[None, None, :], EPS)
    sim = dots / denom
    return sim.transpose(0, 2, 1).reshape(B, -1, H, W)

@@ -1,0 +1,218 @@
+from contextlib import ExitStack
+
+import concourse.bass as bass
+import concourse.mybir as mybir
+import concourse.tile as tile
+from concourse.masks import make_identity
+
+F32 = mybir.dt.float32
+BF16 = mybir.dt.bfloat16
+U32 = mybir.dt.uint32
+U8 = mybir.dt.uint8
+FP8X4 = mybir.dt.float8_e4m3fn_x4
+ALU = mybir.AluOpType
+ACT = mybir.ActivationFunctionType
+
+P = 128
+NB, C, HW, K = 4, 1024, 1024, 1024
+FLOPS = 2 * NB * HW * C * K
+INV_EPS = 1.0e8
+TINY = 1.2e-35
+LEAD = 12
+U_ENGINE = "gggggggg"
+PCOPY_ENGINE = "vvvvvvvv"
+S_UNITS = ()
+
+
+def tile_globalprototype_t_kernel(tc, features, prototypes, out):
+    nc = tc.nc
+    feat = features.rearrange("b c h w -> b c (h w)")
+    outv = out.rearrange("b (p m) h w -> b p m (h w)", m=8)
+    prot = prototypes.rearrange("(p m) c -> p m c", m=8)
+
+    with ExitStack() as ctx:
+        keep = ctx.enter_context(tc.tile_pool(name="keep", bufs=1))
+        work = ctx.enter_context(tc.tile_pool(name="work", bufs=2))
+        psum = ctx.enter_context(tc.psum_pool(name="psum", bufs=1))
+
+        ident = keep.tile([P, P], F32, name="ident", tag="ident")
+        make_identity(nc, ident[:])
+        warm = keep.tile([P, 1], F32, name="warm", tag="warm")
+        nc.vector.memset(warm[:], 1.0)
+        warm2 = keep.tile([P, 1], F32, name="warm2", tag="warm2")
+        nc.scalar.activation(out=warm2[:], in_=warm[:], func=ACT.Sqrt)
+
+        pcodes = keep.tile([P, 8, 2, P], U32, name="pcodes", tag="pcodes", align_bytes=64)
+        pscales = keep.tile([P, 8, 2, P], U8, name="pscales", tag="pscales", align_bytes=64)
+        fcodes = [keep.tile([P, 2, HW], U32, name="fcodes%d" % b, tag="fcodes%d" % b, align_bytes=64) for b in range(NB)]
+        fscales = [keep.tile([P, 2, HW], U8, name="fscales%d" % b, tag="fscales%d" % b, align_bytes=64) for b in range(NB)]
+        rfb = [keep.tile([P, HW], F32, name="rfb%d" % b, tag="rfb%d" % b) for b in range(NB)]
+        ssf = [keep.tile([P, 4, 2, 2], F32, name="ssf%d" % b, tag="ssf%d" % b) for b in range(NB)]
+        ssp = [keep.tile([P, 4], F32, name="ssp%d" % i, tag="ssp%d" % i) for i in range(2)]
+        rp = [keep.tile([P, 4], F32, name="rp%d" % i, tag="rp%d" % i) for i in range(2)]
+
+        praw = [None, None]
+        raw = {}
+
+        def load_p(i):
+            t = work.tile([P, 4, C], BF16, name="praw%d" % i, tag="raw", bufs=8)
+            nc.sync.dma_start(out=t[:], in_=prot[:, 4 * i : 4 * i + 4, :])
+            praw[i] = t
+
+        def load_f(b, g):
+            t = work.tile([P, 4, HW], BF16, name="raw%d%d" % (b, g), tag="raw", bufs=8)
+            nc.sync.dma_start(
+                out=t[:].rearrange("p (u e) x -> p u (e x)", u=2),
+                in_=feat[b, 512 * g : 512 * g + 512, :].rearrange("(u p e) x -> p u (e x)", u=2, e=2),
+            )
+            raw[(b, g)] = t
+
+        load_p(0)
+        load_f(0, 0)
+        load_f(0, 1)
+        load_p(1)
+        for b in range(1, NB):
+            load_f(b, 0)
+            load_f(b, 1)
+
+        def proto_half(i):
+            words = praw[i][:].bitcast(F32)
+            for pair in range(2):
+                pg = work.tile([P, 2, 2, P, 4], BF16, name="pg", tag="pg", bufs=2, align_bytes=64)
+                pgw = pg[:].bitcast(F32)
+                for a in range(2):
+                    mm = 2 * pair + a
+                    m = 4 * i + mm
+                    pjunk = work.tile([P, C], BF16, name="pjunk", tag="pjunk", bufs=2)
+                    nc.scalar.activation(out=pjunk[:], in_=praw[i][:, mm, :], func=ACT.Square,
+                                         accum_out=ssp[i][:, mm : mm + 1])
+                    pt = psum.tile([P, 4, P], F32, name="pt", tag="ft", bufs=3)
+                    for j in range(4):
+                        nc.tensor.transpose(pt[:, j, :], words[:, mm, P * j : P * j + P], ident[:])
+                    src = pt[:].rearrange("p (g u) r -> p g r u", g=2)
+                    if PCOPY_ENGINE[m] == "v":
+                        nc.vector.tensor_copy(out=pgw[:, a], in_=src)
+                    else:
+                        nc.scalar.copy(out=pgw[:, a], in_=src)
+                m0 = 4 * i + 2 * pair
+                nc.vector.quantize_mx(
+                    out=pcodes[:, m0 : m0 + 2].rearrange("p a g r -> p (a g r)").bitcast(FP8X4),
+                    scales=pscales[:, m0 : m0 + 2].rearrange("p a g r -> p (a g r)"),
+                    in_=pg[:].rearrange("p a g r t -> p (a g r t)"),
+                )
+            s4 = work.tile([P, 4], F32, name="s4", tag="s4", bufs=2)
+            nc.vector.tensor_scalar_max(out=s4[:], in0=ssp[i][:], scalar1=TINY)
+            n4 = work.tile([P, 4], F32, name="n4", tag="n4", bufs=2)
+            nc.scalar.activation(out=n4[:], in_=s4[:], func=ACT.Sqrt)
+            nc.vector.reciprocal(out=rp[i][:], in_=n4[:])
+
+        def rq(rho):
+            b, g = rho // 2, rho % 2
+            r = raw[(b, g)]
+            grp = work.tile([P, HW, 4], BF16, name="grp", tag="grp", bufs=3, align_bytes=64)
+            for h in range(2):
+                x0 = 512 * h
+                dst = grp[:, x0 : x0 + 512, :].rearrange("p (c i) t -> p c t i", i=4)
+                src = r[:, :, x0 : x0 + 512].rearrange("p t (c i) -> p c t i", i=4)
+                if (rho, h) in S_UNITS:
+                    nc.scalar.copy(out=dst, in_=src)
+                else:
+                    nc.vector.tensor_copy(out=dst, in_=src)
+            nc.vector.quantize_mx(
+                out=fcodes[b][:, g, :].bitcast(FP8X4),
+                scales=fscales[b][:, g, :],
+                in_=grp[:].rearrange("p x t -> p (x t)"),
+            )
+
+        def ft_bank(beta):
+            b, g, blk = beta // 8, (beta % 8) // 4, beta % 4
+            words = raw[(b, g)][:].bitcast(F32)
+            ft = psum.tile([P, 4, P], F32, name="ft", tag="ft", bufs=3)
+            for t in range(4):
+                nc.tensor.transpose(ft[:, t, :], words[:, t, P * blk : P * blk + P], ident[:])
+            halves = ft[:].bitcast(BF16).rearrange("p t (w e) -> p e t w", e=2)
+            for e in range(2):
+                junk = work.tile([P, 4, P], BF16, name="junk", tag="junk", bufs=2)
+                nc.scalar.activation(out=junk[:], in_=halves[:, e], func=ACT.Square,
+                                     accum_out=ssf[b][:, blk, e, g : g + 1])
+
+        def chain(b):
+            parts = ssf[b][:].rearrange("p k e g -> p (k e) g")
+            s8 = work.tile([P, 8], F32, name="s8", tag="s8", bufs=2)
+            nc.vector.scalar_tensor_tensor(out=s8[:], in0=parts[:, :, 0], scalar=TINY, in1=parts[:, :, 1],
+                                           op0=ALU.max, op1=ALU.add)
+            n8 = work.tile([P, 8], F32, name="n8", tag="n8", bufs=2)
+            nc.scalar.activation(out=n8[:], in_=s8[:], func=ACT.Sqrt)
+            rf8 = work.tile([P, 8], F32, name="rf8", tag="rf8", bufs=2)
+            nc.vector.reciprocal(out=rf8[:], in_=n8[:])
+            for hh in range(2):
+                bc = psum.tile([P, 4, P], F32, name="bc", tag="bc", bufs=1)
+                for j in range(4):
+                    col = 4 * hh + j
+                    nc.tensor.transpose(bc[:, j, :], rf8[:, col : col + 1].to_broadcast([P, P]), ident[:])
+                nc.scalar.copy(
+                    out=rfb[b][:, 512 * hh : 512 * hh + 512].rearrange("p (k q e) -> p k q e", k=2, e=2),
+                    in_=bc[:].rearrange("p (k e) q -> p k q e", k=2),
+                )
+
+        us = {}
+        accs = {}
+
+        def make_u(nu):
+            b, m = nu // 8, nu % 8
+            u = work.tile([P, HW], F32, name="u", tag="u", bufs=5)
+            scal = rp[m // 4][:, m % 4 : m % 4 + 1]
+            if U_ENGINE[m] == "g":
+                nc.gpsimd.tensor_scalar(out=u[:], in0=rfb[b][:], scalar1=scal, scalar2=INV_EPS,
+                                        op0=ALU.mult, op1=ALU.min)
+            elif U_ENGINE[m] == "v":
+                nc.vector.tensor_scalar(out=u[:], in0=rfb[b][:], scalar1=scal, scalar2=INV_EPS,
+                                        op0=ALU.mult, op1=ALU.min)
+            else:
+                nc.scalar.activation(out=u[:], in_=rfb[b][:], func=ACT.Copy, scale=scal)
+            us[nu] = u
+
+        def mx(nu):
+            b, m = nu // 8, nu % 8
+            for h in range(2):
+                acc = psum.tile([P, 512], F32, name="acc", tag="acc", bufs=4)
+                for g in range(2):
+                    nc.tensor.matmul_mx(
+                        out=acc[:],
+                        lhsT=pcodes[:, m, g, :].bitcast(FP8X4),
+                        lhsT_scale=pscales[:, m, g, :],
+                        rhs=fcodes[b][:, g, 512 * h : 512 * h + 512].bitcast(FP8X4),
+                        rhs_scale=fscales[b][:, g, 512 * h : 512 * h + 512],
+                        start=(g == 0),
+                        stop=(g == 1),
+                    )
+                accs[(nu, h)] = acc
+
+        def finish(nu):
+            b, m = nu // 8, nu % 8
+            ot = work.tile([P, HW], F32, name="ot", tag="ot", bufs=5)
+            for h in range(2):
+                nc.vector.scalar_tensor_tensor(
+                    out=ot[:, 512 * h : 512 * h + 512], in0=us[nu][:, 512 * h : 512 * h + 512],
+                    scalar=INV_EPS, in1=accs[(nu, h)][:], op0=ALU.min, op1=ALU.mult)
+            nc.sync.dma_start(out=outv[b, :, m, :], in_=ot[:])
+
+        proto_half(0)
+        rq_slot = dict((rho, (5 * rho) // 2 - LEAD) for rho in range(8))
+        for sigma in range(-LEAD, 32):
+            beta = sigma + LEAD
+            for rho in range(8):
+                if rq_slot[rho] == sigma:
+                    rq(rho)
+            if beta >= 8 and beta % 8 == 0 and beta <= 32:
+                if beta == 8:
+                    proto_half(1)
+                chain(beta // 8 - 1)
+            if beta < 32:
+                ft_bank(beta)
+            if 0 <= sigma + 2 < 32:
+                make_u(sigma + 2)
+            if 0 <= sigma + 1 < 32:
+                mx(sigma + 1)
+            if sigma >= 0:
+                finish(sigma)

@@ -163,8 +163,8 @@ def tile_globalprototype_t_kernel(tc, features, prototypes, out):
             u = work.tile([P, HW], F32, name="u", tag="u", bufs=5)
             scal = rp[m // 4][:, m % 4 : m % 4 + 1]
             if U_ENGINE[m] == "g":
-                nc.gpsimd.tensor_scalar(out=u[:], in0=rfb[b][:], scalar1=scal, scalar2=INV_EPS,
-                                        op0=ALU.mult, op1=ALU.min)
+                nc.gpsimd.tensor_scalar(out=u[:], in0=rfb[b][:], scalar1=scal, scalar2=0.0,
+                                        op0=ALU.mult, op1=ALU.add)
             elif U_ENGINE[m] == "v":
                 nc.vector.tensor_scalar(out=u[:], in0=rfb[b][:], scalar1=scal, scalar2=INV_EPS,
                                         op0=ALU.mult, op1=ALU.min)

@@ -1,8 +1,6 @@
 from contextlib import ExitStack
 
-import concourse.bass as bass
 import concourse.mybir as mybir
-import concourse.tile as tile
 from concourse.masks import make_identity
 
 F32 = mybir.dt.float32
@@ -17,11 +15,20 @@ P = 128
 NB, C, HW, K = 4, 1024, 1024, 1024
 FLOPS = 2 * NB * HW * C * K
 INV_EPS = 1.0e8
-TINY = 1.2e-35
-LEAD = 12
-U_ENGINE = "gggggggg"
-PCOPY_ENGINE = "vvvvvvvv"
-S_UNITS = ()
+TINY = 1.3e-35
+UNITS = 32
+ADD_AT = {5: 1, 11: 2, 18: 3}
+RQ_AT = {3: 4, 6: 5, 9: 6, 12: 7}
+
+
+def banks_at(nu):
+    if nu == 0:
+        return 3
+    return 2 if nu % 2 == 1 else 1
+
+
+def u_engine(nu):
+    return "s" if (nu >= 24 and nu % 2 == 1) else "g"
 
 
 def tile_globalprototype_t_kernel(tc, features, prototypes, out):
@@ -33,14 +40,17 @@ def tile_globalprototype_t_kernel(tc, features, prototypes, out):
     with ExitStack() as ctx:
         keep = ctx.enter_context(tc.tile_pool(name="keep", bufs=1))
         work = ctx.enter_context(tc.tile_pool(name="work", bufs=2))
-        psum = ctx.enter_context(tc.psum_pool(name="psum", bufs=1))
+        psum = ctx.enter_context(tc.psum_pool(name="psum", bufs=4))
+        ctx.enter_context(tc.manual_schedule())
 
         ident = keep.tile([P, P], F32, name="ident", tag="ident")
         make_identity(nc, ident[:])
+        tiny = keep.tile([P, 1], F32, name="tiny", tag="tiny")
+        nc.vector.memset(tiny[:], TINY)
+        one = keep.tile([P, 1], F32, name="one", tag="one")
+        nc.vector.memset(one[:], 1.0)
         warm = keep.tile([P, 1], F32, name="warm", tag="warm")
-        nc.vector.memset(warm[:], 1.0)
-        warm2 = keep.tile([P, 1], F32, name="warm2", tag="warm2")
-        nc.scalar.activation(out=warm2[:], in_=warm[:], func=ACT.Sqrt)
+        nc.scalar.activation(out=warm[:], in_=one[:], func=ACT.Sqrt)
 
         pcodes = keep.tile([P, 8, 2, P], U32, name="pcodes", tag="pcodes", align_bytes=64)
         pscales = keep.tile([P, 8, 2, P], U8, name="pscales", tag="pscales", align_bytes=64)
@@ -51,12 +61,26 @@ def tile_globalprototype_t_kernel(tc, features, prototypes, out):
         ssp = [keep.tile([P, 4], F32, name="ssp%d" % i, tag="ssp%d" % i) for i in range(2)]
         rp = [keep.tile([P, 4], F32, name="rp%d" % i, tag="rp%d" % i) for i in range(2)]
 
-        praw = [None, None]
+        praw = {}
         raw = {}
+        pts = {}
+        pgs = {}
+        grps = {}
+        fts = {}
+        bcs = {}
+        s8s = {}
+        n4s = {}
+        n8s = {}
+        rf8s = {}
+        us = {}
+        accs = {}
 
-        def load_p(i):
+        def load_p(i, pieces):
             t = work.tile([P, 4, C], BF16, name="praw%d" % i, tag="raw", bufs=8)
-            nc.sync.dma_start(out=t[:], in_=prot[:, 4 * i : 4 * i + 4, :])
+            step = 4 // pieces
+            for j in range(pieces):
+                nc.sync.dma_start(out=t[:, step * j : step * j + step, :],
+                                  in_=prot[:, 4 * i + step * j : 4 * i + step * j + step, :])
             praw[i] = t
 
         def load_f(b, g):
@@ -67,107 +91,108 @@ def tile_globalprototype_t_kernel(tc, features, prototypes, out):
             )
             raw[(b, g)] = t
 
-        load_p(0)
-        load_f(0, 0)
-        load_f(0, 1)
-        load_p(1)
-        for b in range(1, NB):
-            load_f(b, 0)
-            load_f(b, 1)
+        def pn(m):
+            pjunk = work.tile([P, C], BF16, name="pjunk", tag="pjunk", bufs=2)
+            nc.scalar.activation(out=pjunk[:], in_=praw[m // 4][:, m % 4, :], func=ACT.Square,
+                                 accum_out=ssp[m // 4][:, m % 4 : m % 4 + 1])
 
-        def proto_half(i):
-            words = praw[i][:].bitcast(F32)
-            for pair in range(2):
-                pg = work.tile([P, 2, 2, P, 4], BF16, name="pg", tag="pg", bufs=2, align_bytes=64)
-                pgw = pg[:].bitcast(F32)
-                for a in range(2):
-                    mm = 2 * pair + a
-                    m = 4 * i + mm
-                    pjunk = work.tile([P, C], BF16, name="pjunk", tag="pjunk", bufs=2)
-                    nc.scalar.activation(out=pjunk[:], in_=praw[i][:, mm, :], func=ACT.Square,
-                                         accum_out=ssp[i][:, mm : mm + 1])
-                    pt = psum.tile([P, 4, P], F32, name="pt", tag="ft", bufs=3)
-                    for j in range(4):
-                        nc.tensor.transpose(pt[:, j, :], words[:, mm, P * j : P * j + P], ident[:])
-                    src = pt[:].rearrange("p (g u) r -> p g r u", g=2)
-                    if PCOPY_ENGINE[m] == "v":
-                        nc.vector.tensor_copy(out=pgw[:, a], in_=src)
-                    else:
-                        nc.scalar.copy(out=pgw[:, a], in_=src)
-                m0 = 4 * i + 2 * pair
-                nc.vector.quantize_mx(
-                    out=pcodes[:, m0 : m0 + 2].rearrange("p a g r -> p (a g r)").bitcast(FP8X4),
-                    scales=pscales[:, m0 : m0 + 2].rearrange("p a g r -> p (a g r)"),
-                    in_=pg[:].rearrange("p a g r t -> p (a g r t)"),
-                )
-            s4 = work.tile([P, 4], F32, name="s4", tag="s4", bufs=2)
-            nc.vector.tensor_scalar_max(out=s4[:], in0=ssp[i][:], scalar1=TINY)
-            n4 = work.tile([P, 4], F32, name="n4", tag="n4", bufs=2)
-            nc.scalar.activation(out=n4[:], in_=s4[:], func=ACT.Sqrt)
-            nc.vector.reciprocal(out=rp[i][:], in_=n4[:])
+        def prs(i):
+            n4s[i] = work.tile([P, 4], F32, name="n4", tag="n4", bufs=2)
+            nc.scalar.activation(out=n4s[i][:], in_=ssp[i][:], func=ACT.Sqrt, bias=tiny[:])
 
-        def rq(rho):
+        def prv(i):
+            nc.vector.reciprocal(out=rp[i][:], in_=n4s[i][:])
+
+        def pt(m):
+            words = praw[m // 4][:].bitcast(F32)
+            t = psum.tile([P, 4, P], F32, name="pt", tag="ring")
+            for j in range(4):
+                nc.tensor.transpose(t[:, j, :], words[:, m % 4, P * j : P * j + P], ident[:])
+            pts[m] = t
+
+        def pc(m):
+            if m % 2 == 0:
+                pgs[m // 2] = work.tile([P, 2, 2, P, 4], BF16, name="pg", tag="pg", bufs=2, align_bytes=64)
+            nc.vector.tensor_copy(out=pgs[m // 2][:].bitcast(F32)[:, m % 2],
+                                  in_=pts[m][:].rearrange("p (g u) r -> p g r u", g=2))
+
+        def pq(m0):
+            nc.vector.quantize_mx(
+                out=pcodes[:, m0 : m0 + 2].rearrange("p a g r -> p (a g r)").bitcast(FP8X4),
+                scales=pscales[:, m0 : m0 + 2].rearrange("p a g r -> p (a g r)"),
+                in_=pgs[m0 // 2][:].rearrange("p a g r t -> p (a g r t)"),
+            )
+
+        def regroup(rho, h):
+            if h == 0:
+                grps[rho] = work.tile([P, HW, 4], BF16, name="grp", tag="grp", bufs=3, align_bytes=64)
+            x0 = 512 * h
+            nc.vector.tensor_copy(
+                out=grps[rho][:, x0 : x0 + 512, :].rearrange("p (c i) t -> p c t i", i=4),
+                in_=raw[(rho // 2, rho % 2)][:, :, x0 : x0 + 512].rearrange("p t (c i) -> p c t i", i=4),
+            )
+
+        def quant(rho):
             b, g = rho // 2, rho % 2
-            r = raw[(b, g)]
-            grp = work.tile([P, HW, 4], BF16, name="grp", tag="grp", bufs=3, align_bytes=64)
-            for h in range(2):
-                x0 = 512 * h
-                dst = grp[:, x0 : x0 + 512, :].rearrange("p (c i) t -> p c t i", i=4)
-                src = r[:, :, x0 : x0 + 512].rearrange("p t (c i) -> p c t i", i=4)
-                if (rho, h) in S_UNITS:
-                    nc.scalar.copy(out=dst, in_=src)
-                else:
-                    nc.vector.tensor_copy(out=dst, in_=src)
             nc.vector.quantize_mx(
                 out=fcodes[b][:, g, :].bitcast(FP8X4),
                 scales=fscales[b][:, g, :],
-                in_=grp[:].rearrange("p x t -> p (x t)"),
+                in_=grps[rho][:].rearrange("p x t -> p (x t)"),
             )
 
-        def ft_bank(beta):
+        def ft(beta):
             b, g, blk = beta // 8, (beta % 8) // 4, beta % 4
             words = raw[(b, g)][:].bitcast(F32)
-            ft = psum.tile([P, 4, P], F32, name="ft", tag="ft", bufs=3)
-            for t in range(4):
-                nc.tensor.transpose(ft[:, t, :], words[:, t, P * blk : P * blk + P], ident[:])
-            halves = ft[:].bitcast(BF16).rearrange("p t (w e) -> p e t w", e=2)
+            t = psum.tile([P, 4, P], F32, name="ft", tag="ring")
+            for j in range(4):
+                nc.tensor.transpose(t[:, j, :], words[:, j, P * blk : P * blk + P], ident[:])
+            fts[beta] = t
+
+        def sq(beta):
+            b, g, blk = beta // 8, (beta % 8) // 4, beta % 4
+            halves = fts[beta][:].bitcast(BF16).rearrange("p t (w e) -> p e t w", e=2)
             for e in range(2):
                 junk = work.tile([P, 4, P], BF16, name="junk", tag="junk", bufs=2)
                 nc.scalar.activation(out=junk[:], in_=halves[:, e], func=ACT.Square,
                                      accum_out=ssf[b][:, blk, e, g : g + 1])
 
-        def chain(b):
+        def add(b):
             parts = ssf[b][:].rearrange("p k e g -> p (k e) g")
             s8 = work.tile([P, 8], F32, name="s8", tag="s8", bufs=2)
             nc.vector.scalar_tensor_tensor(out=s8[:], in0=parts[:, :, 0], scalar=TINY, in1=parts[:, :, 1],
                                            op0=ALU.max, op1=ALU.add)
-            n8 = work.tile([P, 8], F32, name="n8", tag="n8", bufs=2)
-            nc.scalar.activation(out=n8[:], in_=s8[:], func=ACT.Sqrt)
-            rf8 = work.tile([P, 8], F32, name="rf8", tag="rf8", bufs=2)
-            nc.vector.reciprocal(out=rf8[:], in_=n8[:])
+            s8s[b] = s8
+
+        def sr(b):
+            n8s[b] = work.tile([P, 8], F32, name="n8", tag="n8", bufs=2)
+            nc.scalar.activation(out=n8s[b][:], in_=s8s[b][:], func=ACT.Sqrt)
+
+        def rv(b):
+            rf8s[b] = work.tile([P, 8], F32, name="rf8", tag="rf8", bufs=2)
+            nc.vector.reciprocal(out=rf8s[b][:], in_=n8s[b][:])
+
+        def bc(b):
             for hh in range(2):
-                bc = psum.tile([P, 4, P], F32, name="bc", tag="bc", bufs=1)
+                t = psum.tile([P, 4, P], F32, name="bc", tag="ring")
                 for j in range(4):
                     col = 4 * hh + j
-                    nc.tensor.transpose(bc[:, j, :], rf8[:, col : col + 1].to_broadcast([P, P]), ident[:])
+                    nc.tensor.transpose(t[:, j, :], rf8s[b][:, col : col + 1].to_broadcast([P, P]), ident[:])
+                bcs[(b, hh)] = t
+
+        def rc(b):
+            for hh in range(2):
                 nc.scalar.copy(
                     out=rfb[b][:, 512 * hh : 512 * hh + 512].rearrange("p (k q e) -> p k q e", k=2, e=2),
-                    in_=bc[:].rearrange("p (k e) q -> p k q e", k=2),
+                    in_=bcs[(b, hh)][:].rearrange("p (k e) q -> p k q e", k=2),
                 )
-
-        us = {}
-        accs = {}
 
         def make_u(nu):
             b, m = nu // 8, nu % 8
             u = work.tile([P, HW], F32, name="u", tag="u", bufs=5)
             scal = rp[m // 4][:, m % 4 : m % 4 + 1]
-            if U_ENGINE[m] == "g":
+            if u_engine(nu) == "g":
                 nc.gpsimd.tensor_scalar(out=u[:], in0=rfb[b][:], scalar1=scal, scalar2=0.0,
                                         op0=ALU.mult, op1=ALU.add)
-            elif U_ENGINE[m] == "v":
-                nc.vector.tensor_scalar(out=u[:], in0=rfb[b][:], scalar1=scal, scalar2=INV_EPS,
-                                        op0=ALU.mult, op1=ALU.min)
             else:
                 nc.scalar.activation(out=u[:], in_=rfb[b][:], func=ACT.Copy, scale=scal)
             us[nu] = u
@@ -175,7 +200,7 @@ def tile_globalprototype_t_kernel(tc, features, prototypes, out):
         def mx(nu):
             b, m = nu // 8, nu % 8
             for h in range(2):
-                acc = psum.tile([P, 512], F32, name="acc", tag="acc", bufs=4)
+                acc = psum.tile([P, 512], F32, name="acc", tag="acc")
                 for g in range(2):
                     nc.tensor.matmul_mx(
                         out=acc[:],
@@ -197,22 +222,78 @@ def tile_globalprototype_t_kernel(tc, features, prototypes, out):
                     scalar=INV_EPS, in1=accs[(nu, h)][:], op0=ALU.min, op1=ALU.mult)
             nc.sync.dma_start(out=outv[b, :, m, :], in_=ot[:])
 
-        proto_half(0)
-        rq_slot = dict((rho, (5 * rho) // 2 - LEAD) for rho in range(8))
-        for sigma in range(-LEAD, 32):
-            beta = sigma + LEAD
-            for rho in range(8):
-                if rq_slot[rho] == sigma:
-                    rq(rho)
-            if beta >= 8 and beta % 8 == 0 and beta <= 32:
-                if beta == 8:
-                    proto_half(1)
-                chain(beta // 8 - 1)
-            if beta < 32:
-                ft_bank(beta)
-            if 0 <= sigma + 2 < 32:
-                make_u(sigma + 2)
-            if 0 <= sigma + 1 < 32:
-                mx(sigma + 1)
-            if sigma >= 0:
-                finish(sigma)
+        load_p(0, 4)
+        load_f(0, 0)
+        load_f(0, 1)
+        load_f(1, 0)
+        load_f(1, 1)
+        load_p(1, 1)
+        for b in range(2, NB):
+            load_f(b, 0)
+            load_f(b, 1)
+
+        for m in range(4):
+            pt(m)
+            pn(m)
+            pc(m)
+            if m % 2 == 1:
+                pq(m - 1)
+        prs(0)
+        regroup(0, 0)
+        prv(0)
+        regroup(0, 1)
+        for beta in range(8):
+            ft(beta)
+            sq(beta)
+        for rho in range(1, 3):
+            regroup(rho, 0)
+            quant(rho - 1)
+            regroup(rho, 1)
+        regroup(3, 0)
+        quant(2)
+        add(0)
+        regroup(3, 1)
+        mx(0)
+        mx(1)
+        sr(0)
+        rv(0)
+        quant(3)
+        pn(4)
+        bc(0)
+        rc(0)
+        for m in range(5, 8):
+            pn(m)
+        prs(1)
+        for m in range(4, 8):
+            pt(m)
+            pc(m)
+        pq(4)
+        pq(6)
+        make_u(0)
+        make_u(1)
+
+        beta = 8
+        for nu in range(UNITS):
+            fresh = list(range(beta, min(32, beta + banks_at(nu))))
+            beta += len(fresh)
+            for x in fresh:
+                ft(x)
+            if nu == 1:
+                prv(1)
+            if nu in ADD_AT:
+                add(ADD_AT[nu])
+                sr(ADD_AT[nu])
+            if nu - 1 in ADD_AT:
+                rv(ADD_AT[nu - 1])
+                bc(ADD_AT[nu - 1])
+                rc(ADD_AT[nu - 1])
+            for x in fresh:
+                sq(x)
+            finish(nu)
+            if nu + 2 < UNITS:
+                mx(nu + 2)
+                make_u(nu + 2)
+            if nu in RQ_AT:
+                regroup(RQ_AT[nu], 0)
+                regroup(RQ_AT[nu], 1)
+                quant(RQ_AT[nu])

@@ -17,7 +17,7 @@ FLOPS = 2 * NB * HW * C * K
 INV_EPS = 1.0e8
 TINY = 1.3e-35
 UNITS = 32
-ADD_AT = {5: 1, 11: 2, 18: 3}
+ADD_AT = {5: 1, 11: 2, 17: 3}
 RQ_AT = {3: 4, 6: 5, 9: 6, 12: 7}
 
 
@@ -28,7 +28,7 @@ def banks_at(nu):
 
 
 def u_engine(nu):
-    return "s" if (nu >= 24 and nu % 2 == 1) else "g"
+    return "s" if (nu >= 17 and nu % 2 == 1) else "g"
 
 
 def tile_globalprototype_t_kernel(tc, features, prototypes, out):
@@ -105,7 +105,7 @@ def tile_globalprototype_t_kernel(tc, features, prototypes, out):
 
         def pt(m):
             words = praw[m // 4][:].bitcast(F32)
-            t = psum.tile([P, 4, P], F32, name="pt", tag="ring")
+            t = psum.tile([P, 4, P], F32, name="pt", tag="ring", bufs=3)
             for j in range(4):
                 nc.tensor.transpose(t[:, j, :], words[:, m % 4, P * j : P * j + P], ident[:])
             pts[m] = t
@@ -143,7 +143,7 @@ def tile_globalprototype_t_kernel(tc, features, prototypes, out):
         def ft(beta):
             b, g, blk = beta // 8, (beta % 8) // 4, beta % 4
             words = raw[(b, g)][:].bitcast(F32)
-            t = psum.tile([P, 4, P], F32, name="ft", tag="ring")
+            t = psum.tile([P, 4, P], F32, name="ft", tag="ring", bufs=3)
             for j in range(4):
                 nc.tensor.transpose(t[:, j, :], words[:, j, P * blk : P * blk + P], ident[:])
             fts[beta] = t
@@ -173,7 +173,7 @@ def tile_globalprototype_t_kernel(tc, features, prototypes, out):
 
         def bc(b):
             for hh in range(2):
-                t = psum.tile([P, 4, P], F32, name="bc", tag="ring")
+                t = psum.tile([P, 4, P], F32, name="bc", tag="ring", bufs=3)
                 for j in range(4):
                     col = 4 * hh + j
                     nc.tensor.transpose(t[:, j, :], rf8s[b][:, col : col + 1].to_broadcast([P, P]), ident[:])
@@ -188,7 +188,7 @@ def tile_globalprototype_t_kernel(tc, features, prototypes, out):
 
         def make_u(nu):
             b, m = nu // 8, nu % 8
-            u = work.tile([P, HW], F32, name="u", tag="u", bufs=5)
+            u = work.tile([P, HW], F32, name="u", tag="u", bufs=6)
             scal = rp[m // 4][:, m % 4 : m % 4 + 1]
             if u_engine(nu) == "g":
                 nc.gpsimd.tensor_scalar(out=u[:], in0=rfb[b][:], scalar1=scal, scalar2=0.0,
@@ -200,7 +200,7 @@ def tile_globalprototype_t_kernel(tc, features, prototypes, out):
         def mx(nu):
             b, m = nu // 8, nu % 8
             for h in range(2):
-                acc = psum.tile([P, 512], F32, name="acc", tag="acc")
+                acc = psum.tile([P, 512], F32, name="acc", tag="acc", bufs=5)
                 for g in range(2):
                     nc.tensor.matmul_mx(
                         out=acc[:],
@@ -215,12 +215,15 @@ def tile_globalprototype_t_kernel(tc, features, prototypes, out):
 
         def finish(nu):
             b, m = nu // 8, nu % 8
-            ot = work.tile([P, HW], F32, name="ot", tag="ot", bufs=5)
+            ot = work.tile([P, HW], F32, name="ot", tag="ot", bufs=6)
             for h in range(2):
                 nc.vector.scalar_tensor_tensor(
                     out=ot[:, 512 * h : 512 * h + 512], in0=us[nu][:, 512 * h : 512 * h + 512],
                     scalar=INV_EPS, in1=accs[(nu, h)][:], op0=ALU.min, op1=ALU.mult)
-            nc.sync.dma_start(out=outv[b, :, m, :], in_=ot[:])
+                if nu == UNITS - 1:
+                    nc.sync.dma_start(out=outv[b, :, m, 512 * h : 512 * h + 512], in_=ot[:, 512 * h : 512 * h + 512])
+            if nu < UNITS - 1:
+                nc.sync.dma_start(out=outv[b, :, m, :], in_=ot[:])
 
         load_p(0, 4)
         load_f(0, 0)

@@ -117,11 +117,12 @@ def tile_globalprototype_t_kernel(tc, features, prototypes, out):
                                   in_=pts[m][:].rearrange("p (g u) r -> p g r u", g=2))
 
         def pq(m0):
-            nc.vector.quantize_mx(
-                out=pcodes[:, m0 : m0 + 2].rearrange("p a g r -> p (a g r)").bitcast(FP8X4),
-                scales=pscales[:, m0 : m0 + 2].rearrange("p a g r -> p (a g r)"),
-                in_=pgs[m0 // 2][:].rearrange("p a g r t -> p (a g r t)"),
-            )
+            for m in (m0, m0 + 1):
+                nc.vector.quantize_mx(
+                    out=pcodes[:, m].rearrange("p g r -> p (g r)").bitcast(FP8X4),
+                    scales=pscales[:, m].rearrange("p g r -> p (g r)"),
+                    in_=pgs[m0 // 2][:, m % 2].rearrange("p g r t -> p (g r t)"),
+                )
 
         def regroup(rho, h):
             if h == 0:
@@ -132,13 +133,15 @@ def tile_globalprototype_t_kernel(tc, features, prototypes, out):
                 in_=raw[(rho // 2, rho % 2)][:, :, x0 : x0 + 512].rearrange("p t (c i) -> p c t i", i=4),
             )
 
-        def quant(rho):
+        def quant(rho, pieces):
             b, g = rho // 2, rho % 2
-            nc.vector.quantize_mx(
-                out=fcodes[b][:, g, :].bitcast(FP8X4),
-                scales=fscales[b][:, g, :],
-                in_=grps[rho][:].rearrange("p x t -> p (x t)"),
-            )
+            w = HW // pieces
+            for j in range(pieces):
+                nc.vector.quantize_mx(
+                    out=fcodes[b][:, g, w * j : w * j + w].bitcast(FP8X4),
+                    scales=fscales[b][:, g, w * j : w * j + w],
+                    in_=grps[rho][:, w * j : w * j + w, :].rearrange("p x t -> p (x t)"),
+                )
 
         def ft(beta):
             b, g, blk = beta // 8, (beta % 8) // 4, beta % 4
@@ -250,17 +253,17 @@ def tile_globalprototype_t_kernel(tc, features, prototypes, out):
             sq(beta)
         for rho in range(1, 3):
             regroup(rho, 0)
-            quant(rho - 1)
+            quant(rho - 1, 1)
             regroup(rho, 1)
         regroup(3, 0)
-        quant(2)
+        quant(2, 1)
         add(0)
         regroup(3, 1)
         mx(0)
         mx(1)
         sr(0)
         rv(0)
-        quant(3)
+        quant(3, 2)
         pn(4)
         bc(0)
         rc(0)
@@ -299,4 +302,4 @@ def tile_globalprototype_t_kernel(tc, features, prototypes, out):
             if nu in RQ_AT:
                 regroup(RQ_AT[nu], 0)
                 regroup(RQ_AT[nu], 1)
-                quant(RQ_AT[nu])
+                quant(RQ_AT[nu], 2)

@@ -18,7 +18,7 @@ INV_EPS = 1.0e8
 TINY = 1.3e-35
 UNITS = 32
 ADD_AT = {5: 1, 11: 2, 17: 3}
-RQ_AT = {3: 4, 6: 5, 9: 6, 12: 7}
+LATE_FROM = 2
 
 
 def banks_at(nu):
@@ -299,7 +299,9 @@ def tile_globalprototype_t_kernel(tc, features, prototypes, out):
             if nu + 2 < UNITS:
                 mx(nu + 2)
                 make_u(nu + 2)
-            if nu in RQ_AT:
-                regroup(RQ_AT[nu], 0)
-                regroup(RQ_AT[nu], 1)
-                quant(RQ_AT[nu], 2)
+            if LATE_FROM <= nu < LATE_FROM + 12:
+                rho, part = 4 + (nu - LATE_FROM) // 3, (nu - LATE_FROM) % 3
+                if part < 2:
+                    regroup(rho, part)
+                else:
+                    quant(rho, 1)

from contextlib import ExitStack

import concourse.mybir as mybir
from concourse.masks import make_identity

F32 = mybir.dt.float32
BF16 = mybir.dt.bfloat16
U32 = mybir.dt.uint32
U8 = mybir.dt.uint8
FP8X4 = mybir.dt.float8_e4m3fn_x4
ALU = mybir.AluOpType
ACT = mybir.ActivationFunctionType

P = 128
NB, C, HW, K = 4, 1024, 1024, 1024
FLOPS = 2 * NB * HW * C * K
INV_EPS = 1.0e8
TINY = 1.3e-35
UNITS = 32
ADD_AT = {5: 1, 11: 2, 17: 3}
LATE_FROM = 2


def banks_at(nu):
    if nu == 0:
        return 3
    return 2 if nu % 2 == 1 else 1


def u_engine(nu):
    return "s" if (nu >= 17 and nu % 2 == 1) else "g"


def tile_globalprototype_t_kernel(tc, features, prototypes, out):
    nc = tc.nc
    feat = features.rearrange("b c h w -> b c (h w)")
    outv = out.rearrange("b (p m) h w -> b p m (h w)", m=8)
    prot = prototypes.rearrange("(p m) c -> p m c", m=8)

    with ExitStack() as ctx:
        keep = ctx.enter_context(tc.tile_pool(name="keep", bufs=1))
        work = ctx.enter_context(tc.tile_pool(name="work", bufs=2))
        psum = ctx.enter_context(tc.psum_pool(name="psum", bufs=4))
        ctx.enter_context(tc.manual_schedule())

        ident = keep.tile([P, P], F32, name="ident", tag="ident")
        make_identity(nc, ident[:])
        tiny = keep.tile([P, 1], F32, name="tiny", tag="tiny")
        nc.vector.memset(tiny[:], TINY)
        one = keep.tile([P, 1], F32, name="one", tag="one")
        nc.vector.memset(one[:], 1.0)
        warm = keep.tile([P, 1], F32, name="warm", tag="warm")
        nc.scalar.activation(out=warm[:], in_=one[:], func=ACT.Sqrt)

        pcodes = keep.tile([P, 8, 2, P], U32, name="pcodes", tag="pcodes", align_bytes=64)
        pscales = keep.tile([P, 8, 2, P], U8, name="pscales", tag="pscales", align_bytes=64)
        fcodes = [keep.tile([P, 2, HW], U32, name="fcodes%d" % b, tag="fcodes%d" % b, align_bytes=64) for b in range(NB)]
        fscales = [keep.tile([P, 2, HW], U8, name="fscales%d" % b, tag="fscales%d" % b, align_bytes=64) for b in range(NB)]
        rfb = [keep.tile([P, HW], F32, name="rfb%d" % b, tag="rfb%d" % b) for b in range(NB)]
        ssf = [keep.tile([P, 4, 2, 2], F32, name="ssf%d" % b, tag="ssf%d" % b) for b in range(NB)]
        ssp = [keep.tile([P, 4], F32, name="ssp%d" % i, tag="ssp%d" % i) for i in range(2)]
        rp = [keep.tile([P, 4], F32, name="rp%d" % i, tag="rp%d" % i) for i in range(2)]

        praw = {}
        raw = {}
        pts = {}
        pgs = {}
        grps = {}
        fts = {}
        bcs = {}
        s8s = {}
        n4s = {}
        n8s = {}
        rf8s = {}
        us = {}
        accs = {}

        def load_p(i, pieces):
            t = work.tile([P, 4, C], BF16, name="praw%d" % i, tag="raw", bufs=8)
            step = 4 // pieces
            for j in range(pieces):
                nc.sync.dma_start(out=t[:, step * j : step * j + step, :],
                                  in_=prot[:, 4 * i + step * j : 4 * i + step * j + step, :])
            praw[i] = t

        def load_f(b, g):
            t = work.tile([P, 4, HW], BF16, name="raw%d%d" % (b, g), tag="raw", bufs=8)
            nc.sync.dma_start(
                out=t[:].rearrange("p (u e) x -> p u (e x)", u=2),
                in_=feat[b, 512 * g : 512 * g + 512, :].rearrange("(u p e) x -> p u (e x)", u=2, e=2),
            )
            raw[(b, g)] = t

        def pn(m):
            pjunk = work.tile([P, C], BF16, name="pjunk", tag="pjunk", bufs=2)
            nc.scalar.activation(out=pjunk[:], in_=praw[m // 4][:, m % 4, :], func=ACT.Square,
                                 accum_out=ssp[m // 4][:, m % 4 : m % 4 + 1])

        def prs(i):
            n4s[i] = work.tile([P, 4], F32, name="n4", tag="n4", bufs=2)
            nc.scalar.activation(out=n4s[i][:], in_=ssp[i][:], func=ACT.Sqrt, bias=tiny[:])

        def prv(i):
            nc.vector.reciprocal(out=rp[i][:], in_=n4s[i][:])

        def pt(m):
            words = praw[m // 4][:].bitcast(F32)
            t = psum.tile([P, 4, P], F32, name="pt", tag="ring", bufs=3)
            for j in range(4):
                nc.tensor.transpose(t[:, j, :], words[:, m % 4, P * j : P * j + P], ident[:])
            pts[m] = t

        def pc(m):
            if m % 2 == 0:
                pgs[m // 2] = work.tile([P, 2, 2, P, 4], BF16, name="pg", tag="pg", bufs=2, align_bytes=64)
            nc.vector.tensor_copy(out=pgs[m // 2][:].bitcast(F32)[:, m % 2],
                                  in_=pts[m][:].rearrange("p (g u) r -> p g r u", g=2))

        def pq(m0):
            for m in (m0, m0 + 1):
                nc.vector.quantize_mx(
                    out=pcodes[:, m].rearrange("p g r -> p (g r)").bitcast(FP8X4),
                    scales=pscales[:, m].rearrange("p g r -> p (g r)"),
                    in_=pgs[m0 // 2][:, m % 2].rearrange("p g r t -> p (g r t)"),
                )

        def regroup(rho, h):
            if h == 0:
                grps[rho] = work.tile([P, HW, 4], BF16, name="grp", tag="grp", bufs=3, align_bytes=64)
            x0 = 512 * h
            nc.vector.tensor_copy(
                out=grps[rho][:, x0 : x0 + 512, :].rearrange("p (c i) t -> p c t i", i=4),
                in_=raw[(rho // 2, rho % 2)][:, :, x0 : x0 + 512].rearrange("p t (c i) -> p c t i", i=4),
            )

        def quant(rho, pieces):
            b, g = rho // 2, rho % 2
            w = HW // pieces
            for j in range(pieces):
                nc.vector.quantize_mx(
                    out=fcodes[b][:, g, w * j : w * j + w].bitcast(FP8X4),
                    scales=fscales[b][:, g, w * j : w * j + w],
                    in_=grps[rho][:, w * j : w * j + w, :].rearrange("p x t -> p (x t)"),
                )

        def ft(beta):
            b, g, blk = beta // 8, (beta % 8) // 4, beta % 4
            words = raw[(b, g)][:].bitcast(F32)
            t = psum.tile([P, 4, P], F32, name="ft", tag="ring", bufs=3)
            for j in range(4):
                nc.tensor.transpose(t[:, j, :], words[:, j, P * blk : P * blk + P], ident[:])
            fts[beta] = t

        def sq(beta):
            b, g, blk = beta // 8, (beta % 8) // 4, beta % 4
            halves = fts[beta][:].bitcast(BF16).rearrange("p t (w e) -> p e t w", e=2)
            for e in range(2):
                junk = work.tile([P, 4, P], BF16, name="junk", tag="junk", bufs=2)
                nc.scalar.activation(out=junk[:], in_=halves[:, e], func=ACT.Square,
                                     accum_out=ssf[b][:, blk, e, g : g + 1])

        def add(b):
            parts = ssf[b][:].rearrange("p k e g -> p (k e) g")
            s8 = work.tile([P, 8], F32, name="s8", tag="s8", bufs=2)
            nc.vector.scalar_tensor_tensor(out=s8[:], in0=parts[:, :, 0], scalar=TINY, in1=parts[:, :, 1],
                                           op0=ALU.max, op1=ALU.add)
            s8s[b] = s8

        def sr(b):
            n8s[b] = work.tile([P, 8], F32, name="n8", tag="n8", bufs=2)
            nc.scalar.activation(out=n8s[b][:], in_=s8s[b][:], func=ACT.Sqrt)

        def rv(b):
            rf8s[b] = work.tile([P, 8], F32, name="rf8", tag="rf8", bufs=2)
            nc.vector.reciprocal(out=rf8s[b][:], in_=n8s[b][:])

        def bc(b):
            for hh in range(2):
                t = psum.tile([P, 4, P], F32, name="bc", tag="ring", bufs=3)
                for j in range(4):
                    col = 4 * hh + j
                    nc.tensor.transpose(t[:, j, :], rf8s[b][:, col : col + 1].to_broadcast([P, P]), ident[:])
                bcs[(b, hh)] = t

        def rc(b):
            for hh in range(2):
                nc.scalar.copy(
                    out=rfb[b][:, 512 * hh : 512 * hh + 512].rearrange("p (k q e) -> p k q e", k=2, e=2),
                    in_=bcs[(b, hh)][:].rearrange("p (k e) q -> p k q e", k=2),
                )

        def make_u(nu):
            b, m = nu // 8, nu % 8
            u = work.tile([P, HW], F32, name="u", tag="u", bufs=6)
            scal = rp[m // 4][:, m % 4 : m % 4 + 1]
            if u_engine(nu) == "g":
                nc.gpsimd.tensor_scalar(out=u[:], in0=rfb[b][:], scalar1=scal, scalar2=0.0,
                                        op0=ALU.mult, op1=ALU.add)
            else:
                nc.scalar.activation(out=u[:], in_=rfb[b][:], func=ACT.Copy, scale=scal)
            us[nu] = u

        def mx(nu):
            b, m = nu // 8, nu % 8
            for h in range(2):
                acc = psum.tile([P, 512], F32, name="acc", tag="acc", bufs=5)
                for g in range(2):
                    nc.tensor.matmul_mx(
                        out=acc[:],
                        lhsT=pcodes[:, m, g, :].bitcast(FP8X4),
                        lhsT_scale=pscales[:, m, g, :],
                        rhs=fcodes[b][:, g, 512 * h : 512 * h + 512].bitcast(FP8X4),
                        rhs_scale=fscales[b][:, g, 512 * h : 512 * h + 512],
                        start=(g == 0),
                        stop=(g == 1),
                    )
                accs[(nu, h)] = acc

        def finish(nu):
            b, m = nu // 8, nu % 8
            ot = work.tile([P, HW], F32, name="ot", tag="ot", bufs=6)
            for h in range(2):
                nc.vector.scalar_tensor_tensor(
                    out=ot[:, 512 * h : 512 * h + 512], in0=us[nu][:, 512 * h : 512 * h + 512],
                    scalar=INV_EPS, in1=accs[(nu, h)][:], op0=ALU.min, op1=ALU.mult)
                if nu == UNITS - 1:
                    nc.sync.dma_start(out=outv[b, :, m, 512 * h : 512 * h + 512], in_=ot[:, 512 * h : 512 * h + 512])
            if nu < UNITS - 1:
                nc.sync.dma_start(out=outv[b, :, m, :], in_=ot[:])

        load_p(0, 4)
        load_f(0, 0)
        load_f(0, 1)
        load_f(1, 0)
        load_f(1, 1)
        load_p(1, 1)
        for b in range(2, NB):
            load_f(b, 0)
            load_f(b, 1)

        for m in range(4):
            pt(m)
            pn(m)
            pc(m)
            if m % 2 == 1:
                pq(m - 1)
        prs(0)
        regroup(0, 0)
        prv(0)
        regroup(0, 1)
        for beta in range(8):
            ft(beta)
            sq(beta)
        for rho in range(1, 3):
            regroup(rho, 0)
            quant(rho - 1, 1)
            regroup(rho, 1)
        regroup(3, 0)
        quant(2, 1)
        add(0)
        regroup(3, 1)
        mx(0)
        mx(1)
        sr(0)
        rv(0)
        quant(3, 2)
        pn(4)
        bc(0)
        rc(0)
        for m in range(5, 8):
            pn(m)
        prs(1)
        for m in range(4, 8):
            pt(m)
            pc(m)
        pq(4)
        pq(6)
        make_u(0)
        make_u(1)

        beta = 8
        for nu in range(UNITS):
            fresh = list(range(beta, min(32, beta + banks_at(nu))))
            beta += len(fresh)
            for x in fresh:
                ft(x)
            if nu == 1:
                prv(1)
            if nu in ADD_AT:
                add(ADD_AT[nu])
                sr(ADD_AT[nu])
            if nu - 1 in ADD_AT:
                rv(ADD_AT[nu - 1])
                bc(ADD_AT[nu - 1])
                rc(ADD_AT[nu - 1])
            for x in fresh:
                sq(x)
            finish(nu)
            if nu + 2 < UNITS:
                mx(nu + 2)
                make_u(nu + 2)
            if LATE_FROM <= nu < LATE_FROM + 12:
                rho, part = 4 + (nu - LATE_FROM) // 3, (nu - LATE_FROM) % 3
                if part < 2:
                    regroup(rho, part)
                else:
                    quant(rho, 1)
